import numpy as np
import ml_dtypes


def mxq(x, axis, fmt="e4m3"):
    dtype, down = {"e4m3": (ml_dtypes.float8_e4m3fn, 7), "e5m2": (ml_dtypes.float8_e5m2, 14)}[fmt]
    v = np.moveaxis(np.asarray(x, np.float32).astype(ml_dtypes.bfloat16).astype(np.float64), axis, -1)
    blocks = v.reshape(v.shape[:-1] + (-1, 32))
    amax = np.abs(blocks).max(-1, keepdims=True)
    byte = np.maximum(np.where(amax > 0, np.frexp(amax)[1] - 1 + 127, 0) - down, 1)
    scale = np.exp2(byte - 127.0)
    codes = (blocks / scale).astype(np.float32).astype(dtype).astype(np.float64)
    return np.moveaxis((codes * scale).reshape(v.shape), -1, axis)


WIDE = False


def mx_kscale(k):
    if not WIDE:
        return np.ones(k)
    levels = np.array([20, -20, 10, -10, 0])
    a = np.random.permutation(np.resize(levels, k // 512 * 4)).reshape(k // 512, 4)
    idx = np.arange(k)
    return np.exp2(a[idx // 512, idx % 128 // 32])


BF16 = ml_dtypes.bfloat16


def bf(x):
    return np.asarray(x, np.float32).astype(BF16)


def f64(x):
    return np.asarray(x).astype(np.float64)


B, Nb1, Nw1, Nb2x, Nb2y, Nw2x, Nw2y, R, C = 512, 2, 16, 4, 2, 16, 16, 128, 2
J1 = Nb1 * Nb1
K1 = C * Nw1 * Nw1
J3 = Nb2x * Nb2y
L1 = J3 * R
J2 = J3 * J1


def setup_inputs():
    u = mx_kscale(L1)
    x = np.random.standard_normal((B, Nb1 * Nw1 * Nb1 * Nw1, C))
    k1 = np.random.standard_normal((J1, K1, L1)) / np.sqrt(K1) / u[None, None, :]
    b1 = np.random.standard_normal((1, J1, L1)) * 0.3
    gy = np.random.standard_normal((B, J1, J3, R)) * np.exp2(np.random.randint(-12, 1, (B, J1, 1, 1))) * 4.0
    gy = gy * u.reshape(J3, R)[None, None, :, :]
    g = gy.transpose(0, 3, 1, 2).reshape(B, J2, R)
    return {"x": bf(x), "k1": bf(k1), "b1": bf(b1), "grad_out": bf(g)}


def reference(x, k1, b1, grad_out):
    gy = f64(grad_out).reshape(B, R, J1, J3).transpose(2, 0, 3, 1).reshape(J1, B, L1)
    gh = mxq(gy, 2, "e5m2") @ mxq(f64(k1), 2, "e4m3").transpose(0, 2, 1)
    gh = gh.transpose(1, 0, 2).reshape(B, Nb1, Nb1, Nw1, Nw1, C).transpose(0, 1, 3, 2, 4, 5)
    return gh.reshape(B, Nb1 * Nw1 * Nb1 * Nw1, C)

@@ -1,0 +1,131 @@
+from contextlib import ExitStack
+
+import concourse.mybir as mybir
+from concourse.masks import make_identity
+
+BF16 = mybir.dt.bfloat16
+F32 = mybir.dt.float32
+U32 = mybir.dt.uint32
+U8 = mybir.dt.uint8
+E4M3_X4 = mybir.dt.float8_e4m3fn_x4
+E5M2_X4 = mybir.dt.float8_e5m2_x4
+
+P = 128
+PACK = 4
+SAMPLES = 512
+BLOCKS = 4
+WINDOW = 512
+FEATURES = 1024
+GROUPS = FEATURES // P
+PASSES = FEATURES // (P * PACK)
+SAMPLE_TILES = SAMPLES // P
+WINDOW_TILES = WINDOW // P
+RUN = 32
+
+FLOPS = 2 * BLOCKS * SAMPLES * WINDOW * FEATURES
+BYTES = 2 * BLOCKS * WINDOW * FEATURES + 2 * SAMPLES * BLOCKS * FEATURES + 4 * SAMPLES * BLOCKS * WINDOW
+
+
+def tile_switchnet_fstar_pa_kernel(tc, x, k1, b1, grad_out, out):
+    nc = tc.nc
+
+    k1_view = k1.rearrange("j (kt p) l -> j kt p l", p=P)
+    grad_view = grad_out.rearrange("(bt p) a c -> bt p (a c)", p=P)
+    out_view = out.rearrange("(bt p) (br rest) c -> bt br p (rest c)", p=P, br=2)
+
+    with ExitStack() as ctx:
+        const = ctx.enter_context(tc.tile_pool(name="const", bufs=1))
+        loads = ctx.enter_context(tc.tile_pool(name="loads", bufs=1))
+        operands = ctx.enter_context(tc.tile_pool(name="operands", bufs=1))
+        stage = ctx.enter_context(tc.tile_pool(name="stage", bufs=2))
+        results = ctx.enter_context(tc.tile_pool(name="results", bufs=1))
+        k_psum = ctx.enter_context(tc.psum_pool(name="k_psum", bufs=3))
+        g_psum = ctx.enter_context(tc.psum_pool(name="g_psum", bufs=2))
+        acc_psum = ctx.enter_context(tc.psum_pool(name="acc_psum", bufs=3))
+
+        ident_bf16 = const.tile([P, P], BF16)
+        make_identity(nc, ident_bf16[:])
+        ident_f32 = const.tile([P, P], F32)
+        make_identity(nc, ident_f32[:])
+
+        k1_rows = [loads.tile([P, WINDOW_TILES, FEATURES], BF16, name="k1_rows%d" % j) for j in range(BLOCKS)]
+        grad_rows = [loads.tile([P, BLOCKS * FEATURES], BF16, name="grad_rows%d" % bt) for bt in range(SAMPLE_TILES)]
+        k_codes = [operands.tile([P, PASSES, WINDOW], U32, name="k_codes%d" % j, align_bytes=64) for j in range(BLOCKS)]
+        k_scales = [operands.tile([P, PASSES, WINDOW], U8, name="k_scales%d" % j, align_bytes=64) for j in range(BLOCKS)]
+        g_codes = [
+            operands.tile([P, BLOCKS, PASSES * P], U32, name="g_codes%d" % bt, align_bytes=64)
+            for bt in range(SAMPLE_TILES)
+        ]
+        g_scales = [
+            operands.tile([P, BLOCKS, PASSES * P], U8, name="g_scales%d" % bt, align_bytes=64)
+            for bt in range(SAMPLE_TILES)
+        ]
+        out_rows = [results.tile([P, 2, WINDOW // RUN, 2, RUN], F32, name="out_rows%d" % bt) for bt in range(SAMPLE_TILES)]
+
+        for s in range(BLOCKS):
+            for kt in range(WINDOW_TILES):
+                nc.sync.dma_start(out=k1_rows[s][:, kt, :], in_=k1_view[s, kt])
+            nc.sync.dma_start(out=grad_rows[s][:], in_=grad_view[s])
+
+        def transpose_k1(j, kt, k_grouped):
+            for g in range(PASSES):
+                k_bank = k_psum.tile([P, PACK, P], BF16)
+                for t in range(PACK):
+                    m = g * PACK + t
+                    nc.tensor.transpose(k_bank[:, t, :], k1_rows[j][:, kt, m * P : (m + 1) * P], ident_bf16[:])
+                nc.scalar.copy(out=k_grouped[:, g, kt, :, :], in_=k_bank[:].rearrange("p t n -> p n t"))
+
+        def transpose_gy(bt, j):
+            words = grad_rows[bt][:].bitcast(F32).rearrange("p (r q) -> p q r", q=BLOCKS * GROUPS // 2)
+            g_bank = g_psum.tile([P, GROUPS // 2, P], F32)
+            for mm in range(GROUPS // 2):
+                nc.tensor.transpose(g_bank[:, mm, :], words[:, j * (GROUPS // 2) + mm, :], ident_f32[:])
+            g_grouped = stage.tile([P, PASSES * P * PACK], BF16, align_bytes=64)
+            nc.vector.tensor_copy(
+                out=g_grouped[:].bitcast(F32).rearrange("p (g b u) -> p g b u", g=PASSES, u=2),
+                in_=g_bank[:].rearrange("p (g u) b -> p g b u", u=2),
+            )
+            nc.vector.quantize_mx(
+                out=g_codes[bt][:, j, :].bitcast(E5M2_X4),
+                scales=g_scales[bt][:, j, :],
+                in_=g_grouped[:],
+            )
+
+        def prepare(s):
+            k_grouped = stage.tile([P, PASSES, WINDOW_TILES, P, PACK], BF16, align_bytes=64)
+            for i in range(BLOCKS):
+                transpose_k1(s, i, k_grouped)
+                transpose_gy(s, i)
+            for g in range(PASSES):
+                nc.vector.quantize_mx(
+                    out=k_codes[s][:, g, :].bitcast(E4M3_X4),
+                    scales=k_scales[s][:, g, :],
+                    in_=k_grouped[:, g].rearrange("p kt n t -> p (kt n t)"),
+                )
+
+        def multiply(bt, j):
+            br, bc = divmod(j, 2)
+            acc = acc_psum.tile([P, WINDOW], F32)
+            for g in range(PASSES):
+                nc.tensor.matmul_mx(
+                    out=acc[:],
+                    lhsT=g_codes[bt][:, j, g * P : (g + 1) * P].bitcast(E5M2_X4),
+                    lhsT_scale=g_scales[bt][:, j, g * P : (g + 1) * P],
+                    rhs=k_codes[j][:, g, :].bitcast(E4M3_X4),
+                    rhs_scale=k_scales[j][:, g, :],
+                    start=(g == 0),
+                    stop=(g == PASSES - 1),
+                )
+            window_rows = acc[:].rearrange("p (wr w) -> p wr w", w=RUN)
+            if bc == 0:
+                nc.scalar.copy(out=out_rows[bt][:, br, :, bc, :], in_=window_rows)
+            else:
+                nc.vector.tensor_copy(out=out_rows[bt][:, br, :, bc, :], in_=window_rows)
+                nc.sync.dma_start(out=out_view[bt, br], in_=out_rows[bt][:, br].rearrange("p wr bc w -> p (wr bc w)"))
+
+        for s in range(BLOCKS):
+            prepare(s)
+            for bt in range(s):
+                multiply(bt, s)
+            for j in range(s + 1):
+                multiply(s, j)

@@ -39,9 +39,8 @@ def tile_switchnet_fstar_pa_kernel(tc, x, k1, b1, grad_out, out):
         operands = ctx.enter_context(tc.tile_pool(name="operands", bufs=1))
         stage = ctx.enter_context(tc.tile_pool(name="stage", bufs=2))
         results = ctx.enter_context(tc.tile_pool(name="results", bufs=1))
-        k_psum = ctx.enter_context(tc.psum_pool(name="k_psum", bufs=3))
-        g_psum = ctx.enter_context(tc.psum_pool(name="g_psum", bufs=2))
-        acc_psum = ctx.enter_context(tc.psum_pool(name="acc_psum", bufs=3))
+        t_psum = ctx.enter_context(tc.psum_pool(name="t_psum", bufs=4))
+        acc_psum = ctx.enter_context(tc.psum_pool(name="acc_psum", bufs=4))
 
         ident_bf16 = const.tile([P, P], BF16)
         make_identity(nc, ident_bf16[:])
@@ -67,41 +66,45 @@ def tile_switchnet_fstar_pa_kernel(tc, x, k1, b1, grad_out, out):
                 nc.sync.dma_start(out=k1_rows[s][:, kt, :], in_=k1_view[s, kt])
             nc.sync.dma_start(out=grad_rows[s][:], in_=grad_view[s])
 
+        def empty_bank(index, out, in_):
+            if index % 2 == 0:
+                nc.scalar.copy(out=out, in_=in_)
+            else:
+                nc.vector.tensor_copy(out=out, in_=in_)
+
         def transpose_k1(j, kt, k_grouped):
             for g in range(PASSES):
-                k_bank = k_psum.tile([P, PACK, P], BF16)
+                k_bank = t_psum.tile([P, PACK, P], BF16, tag="bank")
                 for t in range(PACK):
                     m = g * PACK + t
                     nc.tensor.transpose(k_bank[:, t, :], k1_rows[j][:, kt, m * P : (m + 1) * P], ident_bf16[:])
-                nc.scalar.copy(out=k_grouped[:, g, kt, :, :], in_=k_bank[:].rearrange("p t n -> p n t"))
+                empty_bank(g, k_grouped[:, g, kt, :, :], k_bank[:].rearrange("p t n -> p n t"))
 
-        def transpose_gy(bt, j):
+        def quantise_k1(j, k_grouped):
+            for g in range(PASSES):
+                nc.vector.quantize_mx(
+                    out=k_codes[j][:, g, :].bitcast(E4M3_X4),
+                    scales=k_scales[j][:, g, :],
+                    in_=k_grouped[:, g].rearrange("p kt n t -> p (kt n t)"),
+                )
+
+        def transpose_gy(bt, j, g_grouped):
             words = grad_rows[bt][:].bitcast(F32).rearrange("p (r q) -> p q r", q=BLOCKS * GROUPS // 2)
-            g_bank = g_psum.tile([P, GROUPS // 2, P], F32)
+            g_bank = t_psum.tile([P, GROUPS // 2, P], F32, tag="bank")
             for mm in range(GROUPS // 2):
                 nc.tensor.transpose(g_bank[:, mm, :], words[:, j * (GROUPS // 2) + mm, :], ident_f32[:])
-            g_grouped = stage.tile([P, PASSES * P * PACK], BF16, align_bytes=64)
-            nc.vector.tensor_copy(
-                out=g_grouped[:].bitcast(F32).rearrange("p (g b u) -> p g b u", g=PASSES, u=2),
-                in_=g_bank[:].rearrange("p (g u) b -> p g b u", u=2),
+            empty_bank(
+                j,
+                g_grouped[:, j, :].bitcast(F32).rearrange("p (g b u) -> p g b u", g=PASSES, u=2),
+                g_bank[:].rearrange("p (g u) b -> p g b u", u=2),
             )
+
+        def quantise_gy(bt, j, g_grouped):
             nc.vector.quantize_mx(
                 out=g_codes[bt][:, j, :].bitcast(E5M2_X4),
                 scales=g_scales[bt][:, j, :],
-                in_=g_grouped[:],
+                in_=g_grouped[:, j, :],
             )
-
-        def prepare(s):
-            k_grouped = stage.tile([P, PASSES, WINDOW_TILES, P, PACK], BF16, align_bytes=64)
-            for i in range(BLOCKS):
-                transpose_k1(s, i, k_grouped)
-                transpose_gy(s, i)
-            for g in range(PASSES):
-                nc.vector.quantize_mx(
-                    out=k_codes[s][:, g, :].bitcast(E4M3_X4),
-                    scales=k_scales[s][:, g, :],
-                    in_=k_grouped[:, g].rearrange("p kt n t -> p (kt n t)"),
-                )
 
         def multiply(bt, j):
             br, bc = divmod(j, 2)
@@ -116,16 +119,32 @@ def tile_switchnet_fstar_pa_kernel(tc, x, k1, b1, grad_out, out):
                     start=(g == 0),
                     stop=(g == PASSES - 1),
                 )
-            window_rows = acc[:].rearrange("p (wr w) -> p wr w", w=RUN)
-            if bc == 0:
-                nc.scalar.copy(out=out_rows[bt][:, br, :, bc, :], in_=window_rows)
-            else:
-                nc.vector.tensor_copy(out=out_rows[bt][:, br, :, bc, :], in_=window_rows)
+            nc.scalar.copy(out=out_rows[bt][:, br, :, bc, :], in_=acc[:].rearrange("p (wr w) -> p wr w", w=RUN))
+            if bc == 1:
                 nc.sync.dma_start(out=out_view[bt, br], in_=out_rows[bt][:, br].rearrange("p wr bc w -> p (wr bc w)"))
 
-        for s in range(BLOCKS):
-            prepare(s)
-            for bt in range(s):
-                multiply(bt, s)
-            for j in range(s + 1):
-                multiply(s, j)
+        def share(products, i):
+            return products[len(products) * i // 4 : len(products) * (i + 1) // 4]
+
+        with tc.manual_schedule():
+            ready = []
+            for s in range(BLOCKS):
+                k_grouped = stage.tile([P, PASSES, WINDOW_TILES, P, PACK], BF16, align_bytes=64)
+                for i in range(WINDOW_TILES):
+                    transpose_k1(s, i, k_grouped)
+                    for bt, j in share(ready, i):
+                        multiply(bt, j)
+                quantise_k1(s, k_grouped)
+                ready = [(bt, s) for bt in range(s)]
+
+                g_grouped = stage.tile([P, BLOCKS, PASSES * P * PACK], BF16, align_bytes=64)
+                for i in range(BLOCKS):
+                    transpose_gy(s, i, g_grouped)
+                    if i > 0:
+                        quantise_gy(s, i - 1, g_grouped)
+                    for bt, j in share(ready, i):
+                        multiply(bt, j)
+                quantise_gy(s, BLOCKS - 1, g_grouped)
+                ready = [(s, j) for j in range(s + 1)]
+            for bt, j in ready:
+                multiply(bt, j)

@@ -21,6 +21,7 @@ PASSES = FEATURES // (P * PACK)
 SAMPLE_TILES = SAMPLES // P
 WINDOW_TILES = WINDOW // P
 RUN = 32
+MATMUL_BLOCKS = 3
 
 FLOPS = 2 * BLOCKS * SAMPLES * WINDOW * FEATURES
 BYTES = 2 * BLOCKS * WINDOW * FEATURES + 2 * SAMPLES * BLOCKS * FEATURES + 4 * SAMPLES * BLOCKS * WINDOW
@@ -74,10 +75,15 @@ def tile_switchnet_fstar_pa_kernel(tc, x, k1, b1, grad_out, out):
 
         def transpose_k1(j, kt, k_grouped):
             for g in range(PASSES):
-                k_bank = t_psum.tile([P, PACK, P], BF16, tag="bank")
+                as_matmul = g == 0 and j < MATMUL_BLOCKS
+                k_bank = t_psum.tile([P, PACK, P], F32 if as_matmul else BF16, tag="bank")
                 for t in range(PACK):
                     m = g * PACK + t
-                    nc.tensor.transpose(k_bank[:, t, :], k1_rows[j][:, kt, m * P : (m + 1) * P], ident_bf16[:])
+                    columns = k1_rows[j][:, kt, m * P : (m + 1) * P]
+                    if as_matmul:
+                        nc.tensor.matmul(k_bank[:, t, :], lhsT=columns, rhs=ident_bf16[:], start=True, stop=True)
+                    else:
+                        nc.tensor.transpose(k_bank[:, t, :], columns, ident_bf16[:])
                 empty_bank(g, k_grouped[:, g, kt, :, :], k_bank[:].rearrange("p t n -> p n t"))
 
         def quantise_k1(j, k_grouped):

@@ -62,10 +62,14 @@ def tile_switchnet_fstar_pa_kernel(tc, x, k1, b1, grad_out, out):
         ]
         out_rows = [results.tile([P, 2, WINDOW // RUN, 2, RUN], F32, name="out_rows%d" % bt) for bt in range(SAMPLE_TILES)]
 
-        for s in range(BLOCKS):
-            for kt in range(WINDOW_TILES):
-                nc.sync.dma_start(out=k1_rows[s][:, kt, :], in_=k1_view[s, kt])
-            nc.sync.dma_start(out=grad_rows[s][:], in_=grad_view[s])
+        steps = [("k1", 0), ("gy", 0), ("k1", 1), ("gy", 1), ("k1", 2), ("k1", 3), ("gy", 2), ("gy", 3)]
+
+        for operand, s in steps:
+            if operand == "k1":
+                for kt in range(WINDOW_TILES):
+                    nc.sync.dma_start(out=k1_rows[s][:, kt, :], in_=k1_view[s, kt])
+            else:
+                nc.sync.dma_start(out=grad_rows[s][:], in_=grad_view[s])
 
         def empty_bank(index, out, in_):
             if index % 2 == 0:
@@ -74,17 +78,16 @@ def tile_switchnet_fstar_pa_kernel(tc, x, k1, b1, grad_out, out):
                 nc.vector.tensor_copy(out=out, in_=in_)
 
         def transpose_k1(j, kt, k_grouped):
+            k_bank = t_psum.tile([P, PASSES, PACK, P], BF16, tag="bank")
             for g in range(PASSES):
-                as_matmul = g == 0 and j < MATMUL_BLOCKS
-                k_bank = t_psum.tile([P, PACK, P], F32 if as_matmul else BF16, tag="bank")
                 for t in range(PACK):
                     m = g * PACK + t
                     columns = k1_rows[j][:, kt, m * P : (m + 1) * P]
-                    if as_matmul:
-                        nc.tensor.matmul(k_bank[:, t, :], lhsT=columns, rhs=ident_bf16[:], start=True, stop=True)
+                    if g == 0 and j < MATMUL_BLOCKS:
+                        nc.tensor.matmul(k_bank[:, g, t, :], lhsT=columns, rhs=ident_bf16[:], start=True, stop=True)
                     else:
-                        nc.tensor.transpose(k_bank[:, t, :], columns, ident_bf16[:])
-                empty_bank(g, k_grouped[:, g, kt, :, :], k_bank[:].rearrange("p t n -> p n t"))
+                        nc.tensor.transpose(k_bank[:, g, t, :], columns, ident_bf16[:])
+            empty_bank(kt, k_grouped[:, :, kt, :, :], k_bank[:].rearrange("p g t n -> p g n t"))
 
         def quantise_k1(j, k_grouped):
             for g in range(PASSES):
@@ -129,28 +132,30 @@ def tile_switchnet_fstar_pa_kernel(tc, x, k1, b1, grad_out, out):
             if bc == 1:
                 nc.sync.dma_start(out=out_view[bt, br], in_=out_rows[bt][:, br].rearrange("p wr bc w -> p (wr bc w)"))
 
-        def share(products, i):
-            return products[len(products) * i // 4 : len(products) * (i + 1) // 4]
-
         with tc.manual_schedule():
             ready = []
-            for s in range(BLOCKS):
-                k_grouped = stage.tile([P, PASSES, WINDOW_TILES, P, PACK], BF16, align_bytes=64)
-                for i in range(WINDOW_TILES):
-                    transpose_k1(s, i, k_grouped)
-                    for bt, j in share(ready, i):
+            blocks_done = 0
+            tiles_done = 0
+            for operand, s in steps:
+                if operand == "k1":
+                    k_grouped = stage.tile([P, PASSES, WINDOW_TILES, P, PACK], BF16, align_bytes=64)
+                    for kt in range(WINDOW_TILES):
+                        transpose_k1(s, kt, k_grouped)
+                    for bt, j in ready:
                         multiply(bt, j)
-                quantise_k1(s, k_grouped)
-                ready = [(bt, s) for bt in range(s)]
-
-                g_grouped = stage.tile([P, BLOCKS, PASSES * P * PACK], BF16, align_bytes=64)
-                for i in range(BLOCKS):
-                    transpose_gy(s, i, g_grouped)
-                    if i > 0:
-                        quantise_gy(s, i - 1, g_grouped)
-                    for bt, j in share(ready, i):
+                    quantise_k1(s, k_grouped)
+                    ready = [(bt, s) for bt in range(tiles_done)]
+                    blocks_done += 1
+                else:
+                    g_grouped = stage.tile([P, BLOCKS, PASSES * P * PACK], BF16, align_bytes=64)
+                    for j in range(BLOCKS):
+                        transpose_gy(s, j, g_grouped)
+                        if j > 0:
+                            quantise_gy(s, j - 1, g_grouped)
+                    for bt, j in ready:
                         multiply(bt, j)
-                quantise_gy(s, BLOCKS - 1, g_grouped)
-                ready = [(s, j) for j in range(s + 1)]
+                    quantise_gy(s, BLOCKS - 1, g_grouped)
+                    ready = [(s, j) for j in range(blocks_done)]
+                    tiles_done += 1
             for bt, j in ready:
                 multiply(bt, j)

@@ -21,7 +21,10 @@ PASSES = FEATURES // (P * PACK)
 SAMPLE_TILES = SAMPLES // P
 WINDOW_TILES = WINDOW // P
 RUN = 32
-MATMUL_BLOCKS = 3
+WORDS = FEATURES // 2 // P
+
+NATURAL = (2, 3,)
+PLAIN = [6,6,0,0]
 
 FLOPS = 2 * BLOCKS * SAMPLES * WINDOW * FEATURES
 BYTES = 2 * BLOCKS * WINDOW * FEATURES + 2 * SAMPLES * BLOCKS * FEATURES + 4 * SAMPLES * BLOCKS * WINDOW
@@ -30,7 +33,7 @@ BYTES = 2 * BLOCKS * WINDOW * FEATURES + 2 * SAMPLES * BLOCKS * FEATURES + 4 * S
 def tile_switchnet_fstar_pa_kernel(tc, x, k1, b1, grad_out, out):
     nc = tc.nc
 
-    k1_view = k1.rearrange("j (kt p) l -> j kt p l", p=P)
+    k1_view = k1.rearrange("j (kt p) l -> j p kt l", p=P)
     grad_view = grad_out.rearrange("(bt p) a c -> bt p (a c)", p=P)
     out_view = out.rearrange("(bt p) (br rest) c -> bt br p (rest c)", p=P, br=2)
 
@@ -39,9 +42,10 @@ def tile_switchnet_fstar_pa_kernel(tc, x, k1, b1, grad_out, out):
         loads = ctx.enter_context(tc.tile_pool(name="loads", bufs=1))
         operands = ctx.enter_context(tc.tile_pool(name="operands", bufs=1))
         stage = ctx.enter_context(tc.tile_pool(name="stage", bufs=2))
+        stage_gy = ctx.enter_context(tc.tile_pool(name="stage_gy", bufs=4))
         results = ctx.enter_context(tc.tile_pool(name="results", bufs=1))
-        t_psum = ctx.enter_context(tc.psum_pool(name="t_psum", bufs=4))
-        acc_psum = ctx.enter_context(tc.psum_pool(name="acc_psum", bufs=4))
+        t_psum = ctx.enter_context(tc.psum_pool(name="t_psum", bufs=5))
+        acc_psum = ctx.enter_context(tc.psum_pool(name="acc_psum", bufs=3))
 
         ident_bf16 = const.tile([P, P], BF16)
         make_identity(nc, ident_bf16[:])
@@ -50,6 +54,9 @@ def tile_switchnet_fstar_pa_kernel(tc, x, k1, b1, grad_out, out):
 
         k1_rows = [loads.tile([P, WINDOW_TILES, FEATURES], BF16, name="k1_rows%d" % j) for j in range(BLOCKS)]
         grad_rows = [loads.tile([P, BLOCKS * FEATURES], BF16, name="grad_rows%d" % bt) for bt in range(SAMPLE_TILES)]
+        turned = [
+            {j: loads.tile([P, FEATURES], BF16, name="turned%d_%d" % (bt, j)) for j in NATURAL} for bt in range(SAMPLE_TILES)
+        ]
         k_codes = [operands.tile([P, PASSES, WINDOW], U32, name="k_codes%d" % j, align_bytes=64) for j in range(BLOCKS)]
         k_scales = [operands.tile([P, PASSES, WINDOW], U8, name="k_scales%d" % j, align_bytes=64) for j in range(BLOCKS)]
         g_codes = [
@@ -62,60 +69,97 @@ def tile_switchnet_fstar_pa_kernel(tc, x, k1, b1, grad_out, out):
         ]
         out_rows = [results.tile([P, 2, WINDOW // RUN, 2, RUN], F32, name="out_rows%d" % bt) for bt in range(SAMPLE_TILES)]
 
-        steps = [("k1", 0), ("gy", 0), ("k1", 1), ("gy", 1), ("k1", 2), ("k1", 3), ("gy", 2), ("gy", 3)]
-
-        for operand, s in steps:
+        for operand, s, parts in [("k1", 0, 4), ("gy", 0, 1), ("k1", 1, 4), ("gy", 1, 1), ("k1", 2, 2), ("gy", 2, 1), ("k1", 3, 2), ("gy", 3, 1)]:
             if operand == "k1":
-                for kt in range(WINDOW_TILES):
-                    nc.sync.dma_start(out=k1_rows[s][:, kt, :], in_=k1_view[s, kt])
+                rows = WINDOW_TILES // parts
+                for part in range(parts):
+                    kt = slice(part * rows, (part + 1) * rows)
+                    nc.sync.dma_start(out=k1_rows[s][:, kt, :], in_=k1_view[s, :, kt, :])
             else:
                 nc.sync.dma_start(out=grad_rows[s][:], in_=grad_view[s])
 
-        def empty_bank(index, out, in_):
-            if index % 2 == 0:
+        def copy_on(engine, out, in_):
+            if engine == "scalar":
                 nc.scalar.copy(out=out, in_=in_)
             else:
                 nc.vector.tensor_copy(out=out, in_=in_)
 
-        def transpose_k1(j, kt, k_grouped):
-            k_bank = t_psum.tile([P, PASSES, PACK, P], BF16, tag="bank")
-            for g in range(PASSES):
-                for t in range(PACK):
-                    m = g * PACK + t
-                    columns = k1_rows[j][:, kt, m * P : (m + 1) * P]
-                    if g == 0 and j < MATMUL_BLOCKS:
-                        nc.tensor.matmul(k_bank[:, g, t, :], lhsT=columns, rhs=ident_bf16[:], start=True, stop=True)
-                    else:
-                        nc.tensor.transpose(k_bank[:, g, t, :], columns, ident_bf16[:])
-            empty_bank(kt, k_grouped[:, :, kt, :, :], k_bank[:].rearrange("p g t n -> p g n t"))
+        def turn_gy(bt, j):
+            copy_on(
+                "vector",
+                turned[bt][j][:].rearrange("p (h m r) -> p h r m", h=PASSES, m=PACK),
+                grad_rows[bt][:].rearrange("p (r j h m) -> p j h r m", j=BLOCKS, h=PASSES, m=PACK)[:, j],
+            )
 
-        def quantise_k1(j, k_grouped):
+        def transpose_words(words, grouped, engine):
+            bank = t_psum.tile([P, WORDS, P], F32, tag="bank")
+            for w in range(WORDS):
+                nc.tensor.transpose(bank[:, w, :], words(w), ident_f32[:])
+            copy_on(
+                engine,
+                grouped,
+                bank[:].rearrange("p (g u) n -> p g n u", u=2),
+            )
+
+        k_grouped = {}
+
+        def transpose_k1(j, kt, engine):
+            if kt == 0:
+                k_grouped[j] = stage.tile([P, PASSES, WINDOW_TILES, P, PACK], BF16, name="k_grouped", align_bytes=64)
+            if j in NATURAL:
+                words = k1_rows[j][:, kt, :].bitcast(F32)
+                transpose_words(
+                    lambda w: words[:, w * P : (w + 1) * P],
+                    k_grouped[j][:].rearrange("p g kt n t -> p (g kt n t)").bitcast(F32).rearrange(
+                        "p (g kt n u) -> p g kt n u", g=PASSES, kt=WINDOW_TILES, u=2
+                    )[:, :, kt],
+                    engine,
+                )
+                return
+            bank = t_psum.tile([P, PASSES, PACK, P], BF16, tag="bank")
+            for m in range(GROUPS):
+                g, t = divmod(m, PACK)
+                columns = k1_rows[j][:, kt, m * P : (m + 1) * P]
+                if m < PLAIN[j]:
+                    nc.tensor.matmul(bank[:, g, t, :], lhsT=columns, rhs=ident_bf16[:], start=True, stop=True)
+                else:
+                    nc.tensor.transpose(bank[:, g, t, :], columns, ident_bf16[:])
+            copy_on(engine, k_grouped[j][:, :, kt, :, :], bank[:].rearrange("p g t n -> p g n t"))
+
+        def quantise_k1(j):
             for g in range(PASSES):
                 nc.vector.quantize_mx(
                     out=k_codes[j][:, g, :].bitcast(E4M3_X4),
                     scales=k_scales[j][:, g, :],
-                    in_=k_grouped[:, g].rearrange("p kt n t -> p (kt n t)"),
+                    in_=k_grouped[j][:, g].rearrange("p kt n t -> p (kt n t)"),
                 )
 
-        def transpose_gy(bt, j, g_grouped):
-            words = grad_rows[bt][:].bitcast(F32).rearrange("p (r q) -> p q r", q=BLOCKS * GROUPS // 2)
-            g_bank = t_psum.tile([P, GROUPS // 2, P], F32, tag="bank")
-            for mm in range(GROUPS // 2):
-                nc.tensor.transpose(g_bank[:, mm, :], words[:, j * (GROUPS // 2) + mm, :], ident_f32[:])
-            empty_bank(
-                j,
-                g_grouped[:, j, :].bitcast(F32).rearrange("p (g b u) -> p g b u", g=PASSES, u=2),
-                g_bank[:].rearrange("p (g u) b -> p g b u", u=2),
+        g_grouped = {}
+
+        def transpose_gy(bt, j, engine):
+            g_grouped[bt, j] = stage_gy.tile([P, PASSES * P * PACK], BF16, name="g_grouped", align_bytes=64)
+            if j in NATURAL:
+                words = turned[bt][j][:].bitcast(F32)
+                columns = lambda w: words[:, w * P : (w + 1) * P]
+            else:
+                words = grad_rows[bt][:].bitcast(F32).rearrange("p (r q) -> p q r", q=BLOCKS * WORDS)
+                columns = lambda w: words[:, j * WORDS + w, :]
+            transpose_words(
+                columns,
+                g_grouped[bt, j][:].bitcast(F32).rearrange("p (g b u) -> p g b u", g=PASSES, u=2),
+                engine,
             )
 
-        def quantise_gy(bt, j, g_grouped):
+        def quantise_gy(bt, j):
             nc.vector.quantize_mx(
                 out=g_codes[bt][:, j, :].bitcast(E5M2_X4),
                 scales=g_scales[bt][:, j, :],
-                in_=g_grouped[:, j, :],
+                in_=g_grouped[bt, j][:],
             )
 
-        def multiply(bt, j):
+        finished = set()
+
+        def multiply(bt, j, engine):
             br, bc = divmod(j, 2)
             acc = acc_psum.tile([P, WINDOW], F32)
             for g in range(PASSES):
@@ -128,34 +172,68 @@ def tile_switchnet_fstar_pa_kernel(tc, x, k1, b1, grad_out, out):
                     start=(g == 0),
                     stop=(g == PASSES - 1),
                 )
-            nc.scalar.copy(out=out_rows[bt][:, br, :, bc, :], in_=acc[:].rearrange("p (wr w) -> p wr w", w=RUN))
-            if bc == 1:
-                nc.sync.dma_start(out=out_view[bt, br], in_=out_rows[bt][:, br].rearrange("p wr bc w -> p (wr bc w)"))
+            finished.add((bt, j))
+            halves = 2 if len(finished) == SAMPLE_TILES * BLOCKS else 1
+            rows = WINDOW // RUN // halves
+            for half in range(halves):
+                wr = slice(half * rows, (half + 1) * rows)
+                copy_on(engine, out_rows[bt][:, br, wr, bc, :], acc[:].rearrange("p (wr w) -> p wr w", w=RUN)[:, wr, :])
+                if (bt, j + 1 - 2 * bc) in finished:
+                    nc.sync.dma_start(
+                        out=out_view[bt, br][:, half * rows * 2 * RUN : (half + 1) * rows * 2 * RUN],
+                        in_=out_rows[bt][:, br, wr].rearrange("p wr bc w -> p (wr bc w)"),
+                    )
 
         with tc.manual_schedule():
-            ready = []
-            blocks_done = 0
-            tiles_done = 0
-            for operand, s in steps:
-                if operand == "k1":
-                    k_grouped = stage.tile([P, PASSES, WINDOW_TILES, P, PACK], BF16, align_bytes=64)
-                    for kt in range(WINDOW_TILES):
-                        transpose_k1(s, kt, k_grouped)
-                    for bt, j in ready:
-                        multiply(bt, j)
-                    quantise_k1(s, k_grouped)
-                    ready = [(bt, s) for bt in range(tiles_done)]
-                    blocks_done += 1
+            banks = []
+            for kind, s, parts in [("k1", 0, range(4)), ("gy", 0, (0, 1)), ("k1", 1, range(4)), ("gy", 0, (2, 3)), ("gy", 1, (0, 1)), ("k1", 2, range(4)), ("gy", 1, (2, 3)), ("k1", 3, range(4)), ("gy", 2, range(4)), ("gy", 3, range(4))]:
+                banks += [(kind, s, part) for part in parts]
+            done = {}
+            waiting = []
+            queued = set()
+            pending = []
+            units = [0]
+
+            def turn(bank):
+                if bank[0] == "gy" and bank[2] in NATURAL:
+                    turn_gy(bank[1], bank[2])
+
+            def issue(job=None):
+                while pending and pending[0][0] <= units[0]:
+                    pending.pop(0)[1]()
+
+            for bank in banks[:5]:
+                turn(bank)
+            for i, (kind, s, part) in enumerate(banks):
+                if i + 5 < len(banks):
+                    turn(banks[i + 5])
+                units[0] += 1
+                engine = "vector" if i % 4 == 3 else "scalar"
+                if kind == "k1":
+                    transpose_k1(s, part, engine)
+                    if part == WINDOW_TILES - 1:
+                        pending.append((units[0] + 2, lambda s=s: quantise_k1(s)))
+                        done["k1", s] = i
                 else:
-                    g_grouped = stage.tile([P, BLOCKS, PASSES * P * PACK], BF16, align_bytes=64)
+                    transpose_gy(s, part, engine)
+                    pending.append((units[0] + 2, lambda s=s, part=part: quantise_gy(s, part)))
+                    done["gy", s, part] = i
+                issue()
+                for bt in range(SAMPLE_TILES):
                     for j in range(BLOCKS):
-                        transpose_gy(s, j, g_grouped)
-                        if j > 0:
-                            quantise_gy(s, j - 1, g_grouped)
-                    for bt, j in ready:
-                        multiply(bt, j)
-                    quantise_gy(s, BLOCKS - 1, g_grouped)
-                    ready = [(s, j) for j in range(blocks_done)]
-                    tiles_done += 1
-            for bt, j in ready:
-                multiply(bt, j)
+                        if max(done.get(("gy", bt, j), i), done.get(("k1", j), i)) + 6 <= i and (bt, j) not in queued:
+                            queued.add((bt, j))
+                            waiting.append((bt, j))
+                if (i + 1) % 2 == 0:
+                    for bt, j in waiting[:2]:
+                        units[0] += 1
+                        issue()
+                        multiply(bt, j, "scalar")
+                        issue()
+                    waiting = waiting[2:]
+            rest = [(bt, j) for bt in range(SAMPLE_TILES) for j in range(BLOCKS) if (bt, j) not in queued]
+            for bt, j in waiting + rest:
+                units[0] += 1
+                issue()
+                multiply(bt, j, "scalar")
+                issue()

@@ -24,7 +24,7 @@ RUN = 32
 WORDS = FEATURES // 2 // P
 
 NATURAL = (2, 3,)
-PLAIN = [6,6,0,0]
+PLAIN = [4,6,0,0]
 
 FLOPS = 2 * BLOCKS * SAMPLES * WINDOW * FEATURES
 BYTES = 2 * BLOCKS * WINDOW * FEATURES + 2 * SAMPLES * BLOCKS * FEATURES + 4 * SAMPLES * BLOCKS * WINDOW
@@ -91,8 +91,10 @@ def tile_switchnet_fstar_pa_kernel(tc, x, k1, b1, grad_out, out):
                 grad_rows[bt][:].rearrange("p (r j h m) -> p j h r m", j=BLOCKS, h=PASSES, m=PACK)[:, j],
             )
 
-        def transpose_words(words, grouped, engine):
+        def transpose_words(words, grouped, engine, warm):
             bank = t_psum.tile([P, WORDS, P], F32, tag="bank")
+            if warm:
+                nc.tensor.matmul(bank[:, 0, :], lhsT=ident_f32[:], rhs=ident_f32[:], start=True, stop=True)
             for w in range(WORDS):
                 nc.tensor.transpose(bank[:, w, :], words(w), ident_f32[:])
             copy_on(
@@ -103,7 +105,7 @@ def tile_switchnet_fstar_pa_kernel(tc, x, k1, b1, grad_out, out):
 
         k_grouped = {}
 
-        def transpose_k1(j, kt, engine):
+        def transpose_k1(j, kt, engine, warm):
             if kt == 0:
                 k_grouped[j] = stage.tile([P, PASSES, WINDOW_TILES, P, PACK], BF16, name="k_grouped", align_bytes=64)
             if j in NATURAL:
@@ -114,6 +116,7 @@ def tile_switchnet_fstar_pa_kernel(tc, x, k1, b1, grad_out, out):
                         "p (g kt n u) -> p g kt n u", g=PASSES, kt=WINDOW_TILES, u=2
                     )[:, :, kt],
                     engine,
+                    warm,
                 )
                 return
             bank = t_psum.tile([P, PASSES, PACK, P], BF16, tag="bank")
@@ -136,7 +139,7 @@ def tile_switchnet_fstar_pa_kernel(tc, x, k1, b1, grad_out, out):
 
         g_grouped = {}
 
-        def transpose_gy(bt, j, engine):
+        def transpose_gy(bt, j, engine, warm):
             g_grouped[bt, j] = stage_gy.tile([P, PASSES * P * PACK], BF16, name="g_grouped", align_bytes=64)
             if j in NATURAL:
                 words = turned[bt][j][:].bitcast(F32)
@@ -148,6 +151,7 @@ def tile_switchnet_fstar_pa_kernel(tc, x, k1, b1, grad_out, out):
                 columns,
                 g_grouped[bt, j][:].bitcast(F32).rearrange("p (g b u) -> p g b u", g=PASSES, u=2),
                 engine,
+                warm,
             )
 
         def quantise_gy(bt, j):
@@ -186,7 +190,7 @@ def tile_switchnet_fstar_pa_kernel(tc, x, k1, b1, grad_out, out):
 
         with tc.manual_schedule():
             banks = []
-            for kind, s, parts in [("k1", 0, range(4)), ("gy", 0, (0, 1)), ("k1", 1, range(4)), ("gy", 0, (2, 3)), ("gy", 1, (0, 1)), ("k1", 2, range(4)), ("gy", 1, (2, 3)), ("k1", 3, range(4)), ("gy", 2, range(4)), ("gy", 3, range(4))]:
+            for kind, s, parts in [("k1", 0, range(4)), ("gy", 0, (0, 1)), ("k1", 1, range(4)), ("gy", 0, (2, 3)), ("gy", 1, (0, 1)), ("gy", 1, (2, 3)), ("k1", 2, range(4)), ("k1", 3, range(4)), ("gy", 2, range(4)), ("gy", 3, range(4))]:
                 banks += [(kind, s, part) for part in parts]
             done = {}
             waiting = []
@@ -202,35 +206,36 @@ def tile_switchnet_fstar_pa_kernel(tc, x, k1, b1, grad_out, out):
                 while pending and pending[0][0] <= units[0]:
                     pending.pop(0)[1]()
 
-            for bank in banks[:5]:
+            for bank in banks[:4]:
                 turn(bank)
             for i, (kind, s, part) in enumerate(banks):
-                if i + 5 < len(banks):
-                    turn(banks[i + 5])
+                if i + 4 < len(banks):
+                    turn(banks[i + 4])
                 units[0] += 1
                 engine = "vector" if i % 4 == 3 else "scalar"
+                warm = i in (12, 14, 16)
                 if kind == "k1":
-                    transpose_k1(s, part, engine)
+                    transpose_k1(s, part, engine, warm)
                     if part == WINDOW_TILES - 1:
-                        pending.append((units[0] + 2, lambda s=s: quantise_k1(s)))
+                        pending.append((units[0] + 3, lambda s=s: quantise_k1(s)))
                         done["k1", s] = i
                 else:
-                    transpose_gy(s, part, engine)
-                    pending.append((units[0] + 2, lambda s=s, part=part: quantise_gy(s, part)))
+                    transpose_gy(s, part, engine, warm)
+                    pending.append((units[0] + 3, lambda s=s, part=part: quantise_gy(s, part)))
                     done["gy", s, part] = i
                 issue()
                 for bt in range(SAMPLE_TILES):
                     for j in range(BLOCKS):
-                        if max(done.get(("gy", bt, j), i), done.get(("k1", j), i)) + 6 <= i and (bt, j) not in queued:
+                        if max(done.get(("gy", bt, j), i), done.get(("k1", j), i)) + 4 <= i and (bt, j) not in queued:
                             queued.add((bt, j))
                             waiting.append((bt, j))
-                if (i + 1) % 2 == 0:
-                    for bt, j in waiting[:2]:
+                if (i + 1) % 4 == 0:
+                    for bt, j in waiting[:3]:
                         units[0] += 1
                         issue()
                         multiply(bt, j, "scalar")
                         issue()
-                    waiting = waiting[2:]
+                    waiting = waiting[3:]
             rest = [(bt, j) for bt in range(SAMPLE_TILES) for j in range(BLOCKS) if (bt, j) not in queued]
             for bt, j in waiting + rest:
                 units[0] += 1

@@ -33,7 +33,7 @@ BYTES = 2 * BLOCKS * WINDOW * FEATURES + 2 * SAMPLES * BLOCKS * FEATURES + 4 * S
 def tile_switchnet_fstar_pa_kernel(tc, x, k1, b1, grad_out, out):
     nc = tc.nc
 
-    k1_view = k1.rearrange("j (kt p) l -> j p kt l", p=P)
+    k1_view = k1.rearrange("j (p kt) l -> j p kt l", p=P)
     grad_view = grad_out.rearrange("(bt p) a c -> bt p (a c)", p=P)
     out_view = out.rearrange("(bt p) (br rest) c -> bt br p (rest c)", p=P, br=2)
 
@@ -69,7 +69,7 @@ def tile_switchnet_fstar_pa_kernel(tc, x, k1, b1, grad_out, out):
         ]
         out_rows = [results.tile([P, 2, WINDOW // RUN, 2, RUN], F32, name="out_rows%d" % bt) for bt in range(SAMPLE_TILES)]
 
-        for operand, s, parts in [("k1", 0, 4), ("gy", 0, 1), ("k1", 1, 4), ("gy", 1, 1), ("k1", 2, 2), ("gy", 2, 1), ("k1", 3, 2), ("gy", 3, 1)]:
+        for operand, s, parts in [("k1", 0, 4), ("gy", 0, 1), ("k1", 1, 2), ("gy", 1, 1), ("k1", 2, 1), ("gy", 2, 1), ("k1", 3, 1), ("gy", 3, 1)]:
             if operand == "k1":
                 rows = WINDOW_TILES // parts
                 for part in range(parts):
@@ -181,7 +181,11 @@ def tile_switchnet_fstar_pa_kernel(tc, x, k1, b1, grad_out, out):
             rows = WINDOW // RUN // halves
             for half in range(halves):
                 wr = slice(half * rows, (half + 1) * rows)
-                copy_on(engine, out_rows[bt][:, br, wr, bc, :], acc[:].rearrange("p (wr w) -> p wr w", w=RUN)[:, wr, :])
+                copy_on(
+                    engine,
+                    out_rows[bt][:, br, wr, bc, :].rearrange("p wr (q kt) -> p wr q kt", kt=WINDOW_TILES),
+                    acc[:].rearrange("p (kt wr q) -> p wr q kt", kt=WINDOW_TILES, wr=WINDOW // RUN)[:, wr],
+                )
                 if (bt, j + 1 - 2 * bc) in finished:
                     nc.sync.dma_start(
                         out=out_view[bt, br][:, half * rows * 2 * RUN : (half + 1) * rows * 2 * RUN],

@@ -42,7 +42,8 @@ def tile_switchnet_fstar_pa_kernel(tc, x, k1, b1, grad_out, out):
         loads = ctx.enter_context(tc.tile_pool(name="loads", bufs=1))
         operands = ctx.enter_context(tc.tile_pool(name="operands", bufs=1))
         stage = ctx.enter_context(tc.tile_pool(name="stage", bufs=2))
-        stage_gy = ctx.enter_context(tc.tile_pool(name="stage_gy", bufs=4))
+        stage_gy = ctx.enter_context(tc.tile_pool(name="stage_gy", bufs=8))
+        spread_pool = ctx.enter_context(tc.tile_pool(name="spread_pool", bufs=1))
         results = ctx.enter_context(tc.tile_pool(name="results", bufs=1))
         t_psum = ctx.enter_context(tc.psum_pool(name="t_psum", bufs=5))
         acc_psum = ctx.enter_context(tc.psum_pool(name="acc_psum", bufs=3))
@@ -69,7 +70,7 @@ def tile_switchnet_fstar_pa_kernel(tc, x, k1, b1, grad_out, out):
         ]
         out_rows = [results.tile([P, 2, WINDOW // RUN, 2, RUN], F32, name="out_rows%d" % bt) for bt in range(SAMPLE_TILES)]
 
-        for operand, s, parts in [("k1", 0, 4), ("gy", 0, 1), ("k1", 1, 2), ("gy", 1, 1), ("k1", 2, 1), ("gy", 2, 1), ("k1", 3, 1), ("gy", 3, 1)]:
+        for operand, s, parts in [("k1", 0, 4), ("gy", 0, 1), ("k1", 1, 2), ("gy", 1, 1), ("k1", 2, 1), ("k1", 3, 1), ("gy", 2, 1), ("gy", 3, 1)]:
             if operand == "k1":
                 rows = WINDOW_TILES // parts
                 for part in range(parts):
@@ -84,6 +85,15 @@ def tile_switchnet_fstar_pa_kernel(tc, x, k1, b1, grad_out, out):
             else:
                 nc.vector.tensor_copy(out=out, in_=in_)
 
+        spread = {}
+
+        def spread_gy(bt, j):
+            spread[bt, j] = spread_pool.tile([P, WORDS, P], F32, name="spread%d_%d" % (bt, j))
+            words = grad_rows[bt][:].bitcast(F32).rearrange("p (r q) -> p r q", q=BLOCKS * WORDS)
+            nc.vector.tensor_copy(
+                out=spread[bt, j][:].rearrange("p w r -> p r w"), in_=words[:, :, j * WORDS : (j + 1) * WORDS]
+            )
+
         def turn_gy(bt, j):
             copy_on(
                 "vector",
@@ -93,8 +103,8 @@ def tile_switchnet_fstar_pa_kernel(tc, x, k1, b1, grad_out, out):
 
         def transpose_words(words, grouped, engine, warm):
             bank = t_psum.tile([P, WORDS, P], F32, tag="bank")
-            if warm:
-                nc.tensor.matmul(bank[:, 0, :], lhsT=ident_f32[:], rhs=ident_f32[:], start=True, stop=True)
+            for w in range(warm):
+                nc.tensor.matmul(bank[:, w, :], lhsT=ident_f32[:], rhs=ident_f32[:], start=True, stop=True)
             for w in range(WORDS):
                 nc.tensor.transpose(bank[:, w, :], words(w), ident_f32[:])
             copy_on(
@@ -120,6 +130,9 @@ def tile_switchnet_fstar_pa_kernel(tc, x, k1, b1, grad_out, out):
                 )
                 return
             bank = t_psum.tile([P, PASSES, PACK, P], BF16, tag="bank")
+            if warm:
+                first = bank[:].rearrange("p g t n -> p (g t n)").bitcast(F32)[:, :P]
+                nc.tensor.matmul(first, lhsT=ident_f32[:], rhs=ident_f32[:], start=True, stop=True)
             for m in range(GROUPS):
                 g, t = divmod(m, PACK)
                 columns = k1_rows[j][:, kt, m * P : (m + 1) * P]
@@ -144,6 +157,8 @@ def tile_switchnet_fstar_pa_kernel(tc, x, k1, b1, grad_out, out):
             if j in NATURAL:
                 words = turned[bt][j][:].bitcast(F32)
                 columns = lambda w: words[:, w * P : (w + 1) * P]
+            elif (bt, j) in spread:
+                columns = lambda w: spread[bt, j][:, w, :]
             else:
                 words = grad_rows[bt][:].bitcast(F32).rearrange("p (r q) -> p q r", q=BLOCKS * WORDS)
                 columns = lambda w: words[:, j * WORDS + w, :]
@@ -205,6 +220,8 @@ def tile_switchnet_fstar_pa_kernel(tc, x, k1, b1, grad_out, out):
             def turn(bank):
                 if bank[0] == "gy" and bank[2] in NATURAL:
                     turn_gy(bank[1], bank[2])
+                elif bank[0] == "gy" and bank[1] == SAMPLE_TILES - 1:
+                    spread_gy(bank[1], bank[2])
 
             def issue(job=None):
                 while pending and pending[0][0] <= units[0]:
@@ -216,16 +233,16 @@ def tile_switchnet_fstar_pa_kernel(tc, x, k1, b1, grad_out, out):
                 if i + 4 < len(banks):
                     turn(banks[i + 4])
                 units[0] += 1
-                engine = "vector" if i % 4 == 3 else "scalar"
-                warm = i in (12, 14, 16)
+                engine = "vector" if i == 0 or i % 4 == 3 else "scalar"
+                warm = 1 if i in (10, 11, 12, 16, 20) else 0
                 if kind == "k1":
                     transpose_k1(s, part, engine, warm)
                     if part == WINDOW_TILES - 1:
-                        pending.append((units[0] + 3, lambda s=s: quantise_k1(s)))
+                        pending.append((units[0] + 2, lambda s=s: quantise_k1(s)))
                         done["k1", s] = i
                 else:
                     transpose_gy(s, part, engine, warm)
-                    pending.append((units[0] + 3, lambda s=s, part=part: quantise_gy(s, part)))
+                    pending.append((units[0] + 2, lambda s=s, part=part: quantise_gy(s, part)))
                     done["gy", s, part] = i
                 issue()
                 for bt in range(SAMPLE_TILES):
@@ -234,15 +251,15 @@ def tile_switchnet_fstar_pa_kernel(tc, x, k1, b1, grad_out, out):
                             queued.add((bt, j))
                             waiting.append((bt, j))
                 if (i + 1) % 4 == 0:
-                    for bt, j in waiting[:3]:
+                    for bt, j in waiting[:4]:
                         units[0] += 1
                         issue()
-                        multiply(bt, j, "scalar")
+                        multiply(bt, j, "vector" if len(finished) >= 10 and len(finished) % 2 == 0 else "scalar")
                         issue()
-                    waiting = waiting[3:]
+                    waiting = waiting[4:]
             rest = [(bt, j) for bt in range(SAMPLE_TILES) for j in range(BLOCKS) if (bt, j) not in queued]
             for bt, j in waiting + rest:
                 units[0] += 1
                 issue()
-                multiply(bt, j, "scalar")
+                multiply(bt, j, "vector" if len(finished) >= 10 and len(finished) % 2 == 0 else "scalar")
                 issue()

from contextlib import ExitStack

import concourse.mybir as mybir
from concourse.masks import make_identity

BF16 = mybir.dt.bfloat16
F32 = mybir.dt.float32
U32 = mybir.dt.uint32
U8 = mybir.dt.uint8
E4M3_X4 = mybir.dt.float8_e4m3fn_x4
E5M2_X4 = mybir.dt.float8_e5m2_x4

P = 128
PACK = 4
SAMPLES = 512
BLOCKS = 4
WINDOW = 512
FEATURES = 1024
GROUPS = FEATURES // P
PASSES = FEATURES // (P * PACK)
SAMPLE_TILES = SAMPLES // P
WINDOW_TILES = WINDOW // P
RUN = 32
WORDS = FEATURES // 2 // P

NATURAL = (2, 3,)
PLAIN = [4,6,0,0]

FLOPS = 2 * BLOCKS * SAMPLES * WINDOW * FEATURES
BYTES = 2 * BLOCKS * WINDOW * FEATURES + 2 * SAMPLES * BLOCKS * FEATURES + 4 * SAMPLES * BLOCKS * WINDOW


def tile_switchnet_fstar_pa_kernel(tc, x, k1, b1, grad_out, out):
    nc = tc.nc

    k1_view = k1.rearrange("j (p kt) l -> j p kt l", p=P)
    grad_view = grad_out.rearrange("(bt p) a c -> bt p (a c)", p=P)
    out_view = out.rearrange("(bt p) (br rest) c -> bt br p (rest c)", p=P, br=2)

    with ExitStack() as ctx:
        const = ctx.enter_context(tc.tile_pool(name="const", bufs=1))
        loads = ctx.enter_context(tc.tile_pool(name="loads", bufs=1))
        operands = ctx.enter_context(tc.tile_pool(name="operands", bufs=1))
        stage = ctx.enter_context(tc.tile_pool(name="stage", bufs=2))
        stage_gy = ctx.enter_context(tc.tile_pool(name="stage_gy", bufs=8))
        spread_pool = ctx.enter_context(tc.tile_pool(name="spread_pool", bufs=1))
        results = ctx.enter_context(tc.tile_pool(name="results", bufs=1))
        t_psum = ctx.enter_context(tc.psum_pool(name="t_psum", bufs=5))
        acc_psum = ctx.enter_context(tc.psum_pool(name="acc_psum", bufs=3))

        ident_bf16 = const.tile([P, P], BF16)
        make_identity(nc, ident_bf16[:])
        ident_f32 = const.tile([P, P], F32)
        make_identity(nc, ident_f32[:])

        k1_rows = [loads.tile([P, WINDOW_TILES, FEATURES], BF16, name="k1_rows%d" % j) for j in range(BLOCKS)]
        grad_rows = [loads.tile([P, BLOCKS * FEATURES], BF16, name="grad_rows%d" % bt) for bt in range(SAMPLE_TILES)]
        turned = [
            {j: loads.tile([P, FEATURES], BF16, name="turned%d_%d" % (bt, j)) for j in NATURAL} for bt in range(SAMPLE_TILES)
        ]
        k_codes = [operands.tile([P, PASSES, WINDOW], U32, name="k_codes%d" % j, align_bytes=64) for j in range(BLOCKS)]
        k_scales = [operands.tile([P, PASSES, WINDOW], U8, name="k_scales%d" % j, align_bytes=64) for j in range(BLOCKS)]
        g_codes = [
            operands.tile([P, BLOCKS, PASSES * P], U32, name="g_codes%d" % bt, align_bytes=64)
            for bt in range(SAMPLE_TILES)
        ]
        g_scales = [
            operands.tile([P, BLOCKS, PASSES * P], U8, name="g_scales%d" % bt, align_bytes=64)
            for bt in range(SAMPLE_TILES)
        ]
        out_rows = [results.tile([P, 2, WINDOW // RUN, 2, RUN], F32, name="out_rows%d" % bt) for bt in range(SAMPLE_TILES)]

        for operand, s, parts in [("k1", 0, 4), ("gy", 0, 1), ("k1", 1, 2), ("gy", 1, 1), ("k1", 2, 1), ("k1", 3, 1), ("gy", 2, 1), ("gy", 3, 1)]:
            if operand == "k1":
                rows = WINDOW_TILES // parts
                for part in range(parts):
                    kt = slice(part * rows, (part + 1) * rows)
                    nc.sync.dma_start(out=k1_rows[s][:, kt, :], in_=k1_view[s, :, kt, :])
            else:
                nc.sync.dma_start(out=grad_rows[s][:], in_=grad_view[s])

        def copy_on(engine, out, in_):
            if engine == "scalar":
                nc.scalar.copy(out=out, in_=in_)
            else:
                nc.vector.tensor_copy(out=out, in_=in_)

        spread = {}

        def spread_gy(bt, j):
            spread[bt, j] = spread_pool.tile([P, WORDS, P], F32, name="spread%d_%d" % (bt, j))
            words = grad_rows[bt][:].bitcast(F32).rearrange("p (r q) -> p r q", q=BLOCKS * WORDS)
            nc.vector.tensor_copy(
                out=spread[bt, j][:].rearrange("p w r -> p r w"), in_=words[:, :, j * WORDS : (j + 1) * WORDS]
            )

        def turn_gy(bt, j):
            copy_on(
                "vector",
                turned[bt][j][:].rearrange("p (h m r) -> p h r m", h=PASSES, m=PACK),
                grad_rows[bt][:].rearrange("p (r j h m) -> p j h r m", j=BLOCKS, h=PASSES, m=PACK)[:, j],
            )

        def transpose_words(words, grouped, engine, warm):
            bank = t_psum.tile([P, WORDS, P], F32, tag="bank")
            for w in range(warm):
                nc.tensor.matmul(bank[:, w, :], lhsT=ident_f32[:], rhs=ident_f32[:], start=True, stop=True)
            for w in range(WORDS):
                nc.tensor.transpose(bank[:, w, :], words(w), ident_f32[:])
            copy_on(
                engine,
                grouped,
                bank[:].rearrange("p (g u) n -> p g n u", u=2),
            )

        k_grouped = {}

        def transpose_k1(j, kt, engine, warm):
            if kt == 0:
                k_grouped[j] = stage.tile([P, PASSES, WINDOW_TILES, P, PACK], BF16, name="k_grouped", align_bytes=64)
            if j in NATURAL:
                words = k1_rows[j][:, kt, :].bitcast(F32)
                transpose_words(
                    lambda w: words[:, w * P : (w + 1) * P],
                    k_grouped[j][:].rearrange("p g kt n t -> p (g kt n t)").bitcast(F32).rearrange(
                        "p (g kt n u) -> p g kt n u", g=PASSES, kt=WINDOW_TILES, u=2
                    )[:, :, kt],
                    engine,
                    warm,
                )
                return
            bank = t_psum.tile([P, PASSES, PACK, P], BF16, tag="bank")
            if warm:
                first = bank[:].rearrange("p g t n -> p (g t n)").bitcast(F32)[:, :P]
                nc.tensor.matmul(first, lhsT=ident_f32[:], rhs=ident_f32[:], start=True, stop=True)
            for m in range(GROUPS):
                g, t = divmod(m, PACK)
                columns = k1_rows[j][:, kt, m * P : (m + 1) * P]
                if m < PLAIN[j]:
                    nc.tensor.matmul(bank[:, g, t, :], lhsT=columns, rhs=ident_bf16[:], start=True, stop=True)
                else:
                    nc.tensor.transpose(bank[:, g, t, :], columns, ident_bf16[:])
            copy_on(engine, k_grouped[j][:, :, kt, :, :], bank[:].rearrange("p g t n -> p g n t"))

        def quantise_k1(j):
            for g in range(PASSES):
                nc.vector.quantize_mx(
                    out=k_codes[j][:, g, :].bitcast(E4M3_X4),
                    scales=k_scales[j][:, g, :],
                    in_=k_grouped[j][:, g].rearrange("p kt n t -> p (kt n t)"),
                )

        g_grouped = {}

        def transpose_gy(bt, j, engine, warm):
            g_grouped[bt, j] = stage_gy.tile([P, PASSES * P * PACK], BF16, name="g_grouped", align_bytes=64)
            if j in NATURAL:
                words = turned[bt][j][:].bitcast(F32)
                columns = lambda w: words[:, w * P : (w + 1) * P]
            elif (bt, j) in spread:
                columns = lambda w: spread[bt, j][:, w, :]
            else:
                words = grad_rows[bt][:].bitcast(F32).rearrange("p (r q) -> p q r", q=BLOCKS * WORDS)
                columns = lambda w: words[:, j * WORDS + w, :]
            transpose_words(
                columns,
                g_grouped[bt, j][:].bitcast(F32).rearrange("p (g b u) -> p g b u", g=PASSES, u=2),
                engine,
                warm,
            )

        def quantise_gy(bt, j):
            nc.vector.quantize_mx(
                out=g_codes[bt][:, j, :].bitcast(E5M2_X4),
                scales=g_scales[bt][:, j, :],
                in_=g_grouped[bt, j][:],
            )

        finished = set()

        def multiply(bt, j, engine):
            br, bc = divmod(j, 2)
            acc = acc_psum.tile([P, WINDOW], F32)
            for g in range(PASSES):
                nc.tensor.matmul_mx(
                    out=acc[:],
                    lhsT=g_codes[bt][:, j, g * P : (g + 1) * P].bitcast(E5M2_X4),
                    lhsT_scale=g_scales[bt][:, j, g * P : (g + 1) * P],
                    rhs=k_codes[j][:, g, :].bitcast(E4M3_X4),
                    rhs_scale=k_scales[j][:, g, :],
                    start=(g == 0),
                    stop=(g == PASSES - 1),
                )
            finished.add((bt, j))
            halves = 2 if len(finished) == SAMPLE_TILES * BLOCKS else 1
            rows = WINDOW // RUN // halves
            for half in range(halves):
                wr = slice(half * rows, (half + 1) * rows)
                copy_on(
                    engine,
                    out_rows[bt][:, br, wr, bc, :].rearrange("p wr (q kt) -> p wr q kt", kt=WINDOW_TILES),
                    acc[:].rearrange("p (kt wr q) -> p wr q kt", kt=WINDOW_TILES, wr=WINDOW // RUN)[:, wr],
                )
                if (bt, j + 1 - 2 * bc) in finished:
                    nc.sync.dma_start(
                        out=out_view[bt, br][:, half * rows * 2 * RUN : (half + 1) * rows * 2 * RUN],
                        in_=out_rows[bt][:, br, wr].rearrange("p wr bc w -> p (wr bc w)"),
                    )

        with tc.manual_schedule():
            banks = []
            for kind, s, parts in [("k1", 0, range(4)), ("gy", 0, (0, 1)), ("k1", 1, range(4)), ("gy", 0, (2, 3)), ("gy", 1, (0, 1)), ("gy", 1, (2, 3)), ("k1", 2, range(4)), ("k1", 3, range(4)), ("gy", 2, range(4)), ("gy", 3, range(4))]:
                banks += [(kind, s, part) for part in parts]
            done = {}
            waiting = []
            queued = set()
            pending = []
            units = [0]

            def turn(bank):
                if bank[0] == "gy" and bank[2] in NATURAL:
                    turn_gy(bank[1], bank[2])
                elif bank[0] == "gy" and bank[1] == SAMPLE_TILES - 1:
                    spread_gy(bank[1], bank[2])

            def issue(job=None):
                while pending and pending[0][0] <= units[0]:
                    pending.pop(0)[1]()

            for bank in banks[:4]:
                turn(bank)
            for i, (kind, s, part) in enumerate(banks):
                if i + 4 < len(banks):
                    turn(banks[i + 4])
                units[0] += 1
                engine = "vector" if i == 0 or i % 4 == 3 else "scalar"
                warm = 1 if i in (10, 11, 12, 16, 20) else 0
                if kind == "k1":
                    transpose_k1(s, part, engine, warm)
                    if part == WINDOW_TILES - 1:
                        pending.append((units[0] + 2, lambda s=s: quantise_k1(s)))
                        done["k1", s] = i
                else:
                    transpose_gy(s, part, engine, warm)
                    pending.append((units[0] + 2, lambda s=s, part=part: quantise_gy(s, part)))
                    done["gy", s, part] = i
                issue()
                for bt in range(SAMPLE_TILES):
                    for j in range(BLOCKS):
                        if max(done.get(("gy", bt, j), i), done.get(("k1", j), i)) + 4 <= i and (bt, j) not in queued:
                            queued.add((bt, j))
                            waiting.append((bt, j))
                if (i + 1) % 4 == 0:
                    for bt, j in waiting[:4]:
                        units[0] += 1
                        issue()
                        multiply(bt, j, "vector" if len(finished) >= 10 and len(finished) % 2 == 0 else "scalar")
                        issue()
                    waiting = waiting[4:]
            rest = [(bt, j) for bt in range(SAMPLE_TILES) for j in range(BLOCKS) if (bt, j) not in queued]
            for bt, j in waiting + rest:
                units[0] += 1
                issue()
                multiply(bt, j, "vector" if len(finished) >= 10 and len(finished) % 2 == 0 else "scalar")
                issue()
